import numpy as np
import ml_dtypes


def mxq(x, axis, fmt="e4m3"):
    dtype, down = {"e4m3": (ml_dtypes.float8_e4m3fn, 7), "e5m2": (ml_dtypes.float8_e5m2, 14)}[fmt]
    v = np.moveaxis(np.asarray(x, np.float32).astype(ml_dtypes.bfloat16).astype(np.float64), axis, -1)
    blocks = v.reshape(v.shape[:-1] + (-1, 32))
    amax = np.abs(blocks).max(-1, keepdims=True)
    byte = np.maximum(np.where(amax > 0, np.frexp(amax)[1] - 1 + 127, 0) - down, 1)
    scale = np.exp2(byte - 127.0)
    codes = (blocks / scale).astype(np.float32).astype(dtype).astype(np.float64)
    return np.moveaxis((codes * scale).reshape(v.shape), -1, axis)


WIDE = False


def mx_kscale(k):
    if not WIDE:
        return np.ones(k)
    levels = np.array([10, -10, 5, -5, 0])
    if k % 512:
        return np.exp2(np.random.permutation(np.resize(levels, k // 32))).repeat(32)
    a = np.empty((k // 512, 16))
    for p in range(k // 512):
        a[p, :8] = np.random.permutation(np.resize(levels, 8))
        for g in range(8):
            far = levels[np.abs(levels - a[p, g]) >= 10]
            a[p, g + 8] = far[np.random.randint(len(far))]
    return np.exp2(a.ravel()).repeat(32)


BF16 = ml_dtypes.bfloat16


def bf(x):
    return np.asarray(x, np.float32).astype(BF16)


def f64(x):
    return np.asarray(x).astype(np.float64)


B, S, D, QK, EXP = 16, 512, 1024, 32, 32
EPS = 1e-5
W = QK + QK + EXP + EXP
NT = 110


def erf(v):
    a = np.minimum(np.abs(v), 6.0)
    c = 2.0 * a * a
    term = a.copy()
    total = a.copy()
    for n in range(1, NT):
        term = term * c / (2.0 * n + 1.0)
        total = total + term
    return np.sign(v) * (2.0 / np.sqrt(np.pi)) * np.exp(-a * a) * total


def gelu(v):
    return 0.5 * v * (1.0 + erf(v / np.sqrt(2.0)))


def setup_inputs():
    s = mx_kscale(D)
    row_gain = np.exp(0.5 * np.random.standard_normal((B, S)))[..., None]
    row_shift = 0.5 * np.random.standard_normal((B, S))[..., None]
    return {"x": bf(np.random.standard_normal((B, S, D)) * row_gain + row_shift),
            "ln_gamma": bf((1.0 + 0.1 * np.random.standard_normal(D)) * s),
            "ln_beta": bf(0.1 * np.random.standard_normal(D) * s),
            "expand": bf(np.random.standard_normal((W, D)) / np.sqrt(D) / s[None, :])}


def reference(x, ln_gamma, ln_beta, expand):
    x = f64(x)
    mu = x.mean(-1, keepdims=True)
    var = x.var(-1, keepdims=True)
    h = (x - mu) / np.sqrt(var + EPS) * f64(ln_gamma) + f64(ln_beta)
    fused = mxq(h, 2, "e4m3") @ mxq(f64(expand), 1, "e4m3").T
    query = fused[..., :QK]
    key = fused[..., QK:QK + QK]
    linear = fused[..., QK + QK:QK + QK + EXP]
    pre_gelu = fused[..., QK + QK + EXP:]
    geglu = linear * gelu(pre_gelu)
    return query, key, geglu

@@ -1,0 +1,234 @@
+from contextlib import ExitStack
+
+import concourse.mybir as mybir
+from concourse.masks import make_identity
+
+F32 = mybir.dt.float32
+BF16 = mybir.dt.bfloat16
+U32 = mybir.dt.uint32
+U8 = mybir.dt.uint8
+I32 = mybir.dt.int32
+FP8X4 = mybir.dt.float8_e4m3fn_x4
+ALU = mybir.AluOpType
+ACT = mybir.ActivationFunctionType
+
+P = 128
+ROWS = 16 * 512
+D = 1024
+W = 128
+QK = 32
+EPS = 1e-5
+PACK = 4
+RUN = 8
+K_PASS = P * PACK
+PASSES = D // K_PASS
+CHUNKS = D // P
+BN_MAX = 512
+TILES = 4
+GROUP_COLS = TILES * P
+ROWS_PER_PARTITION = ROWS // P
+GROUPS = ROWS_PER_PARTITION // TILES
+X_BUFS = 4
+STAGE_BUFS = 3
+
+FLOPS = 2 * ROWS * D * W
+
+
+def feature_view(row):
+    return row.rearrange("p (q t r) -> p t q r", t=PACK, r=RUN)
+
+
+def sorted_view(row):
+    return row.rearrange("p (t q r) -> p t q r", t=PACK, r=RUN)
+
+
+def chunk_cols(g, t):
+    first = t * (D // PACK) + g * P
+    return slice(first, first + P)
+
+
+def tile_latentattentionblock_pa_t_kernel(tc, x, ln_gamma, ln_beta, expand, out_0, out_1, out_2):
+    nc = tc.nc
+    x_rows = x.flatten_outer_dims().rearrange("(p j) d -> p j d", p=P)
+    out_rows = [o.flatten_outer_dims().rearrange("(p j) c -> p j c", p=P) for o in (out_0, out_1, out_2)]
+
+    with ExitStack() as stack:
+        const = stack.enter_context(tc.tile_pool(name="const", bufs=1))
+
+        ident_f32 = const.tile([P, P], F32)
+        make_identity(nc, ident_f32[:])
+        ident_bf16 = const.tile([P, P], BF16)
+        make_identity(nc, ident_bf16[:])
+        minus_half = const.tile([P, TILES], F32)
+        nc.gpsimd.memset(minus_half[:], -0.5)
+
+        vec_rows = const.tile([P, P], BF16)
+        nc.vector.memset(vec_rows[:].bitcast(I32), 0)
+        for v, vec in enumerate((ln_gamma, ln_beta)):
+            vec_view = vec.rearrange("(g b t r) -> g t b r", g=PASSES, t=PACK, r=RUN)
+            for g in range(PASSES):
+                row = v * CHUNKS + g * PACK
+                nc.scalar.dma_start(
+                    out=vec_rows[row : row + PACK, :].rearrange("t (b r) -> t b r", r=RUN), in_=vec_view[g]
+                )
+        expand_sb = const.tile([W, D], BF16)
+        nc.scalar.dma_start(out=expand_sb[:], in_=expand)
+        expand_sorted = const.tile([W, D], BF16)
+        nc.vector.tensor_copy(out=sorted_view(expand_sorted[:]), in_=feature_view(expand_sb[:]))
+
+        gain_shift = const.tile([P, 2 * CHUNKS], F32)
+        e_grouped = const.tile([P, PASSES, W, PACK], BF16, align_bytes=64)
+        e_codes = const.tile([P, PASSES, W], U32, align_bytes=64)
+        e_scales = const.tile([P, PASSES, W], U8, align_bytes=64)
+        with tc.psum_pool(name="setup_psum", bufs=1) as setup_psum:
+            vec_cols = setup_psum.tile([P, P], BF16)
+            nc.tensor.transpose(vec_cols[:], vec_rows[:], ident_bf16[:])
+            nc.vector.tensor_copy(out=gain_shift[:], in_=vec_cols[:, 0 : 2 * CHUNKS])
+            for g in range(PASSES):
+                e_t = setup_psum.tile([P, PACK, W], BF16, name="e_t%d" % g)
+                for t in range(PACK):
+                    nc.tensor.transpose(e_t[:, t, :], expand_sorted[:, chunk_cols(g, t)], ident_bf16[:])
+                nc.vector.tensor_copy(out=e_grouped[:, g, :, :], in_=e_t[:].rearrange("p t o -> p o t"))
+            nc.vector.quantize_mx(
+                out=e_codes[:].rearrange("p g o -> p (g o)").bitcast(FP8X4),
+                scales=e_scales[:].rearrange("p g o -> p (g o)"),
+                in_=e_grouped[:].rearrange("p g o t -> p (g o t)"),
+            )
+
+        x_pool = stack.enter_context(tc.tile_pool(name="x_pool", bufs=X_BUFS))
+        small = stack.enter_context(tc.tile_pool(name="small", bufs=STAGE_BUFS))
+        work = stack.enter_context(tc.tile_pool(name="work", bufs=STAGE_BUFS))
+        out_pool = stack.enter_context(tc.tile_pool(name="out_pool", bufs=STAGE_BUFS))
+        xt_psum = stack.enter_context(tc.psum_pool(name="xt_psum", bufs=6))
+        acc_psum = stack.enter_context(tc.psum_pool(name="acc_psum", bufs=2))
+
+        live = {}
+
+        def load(i):
+            x_sb = x_pool.tile([P, TILES, D], BF16, name="x_sb")
+            nc.sync.dma_start(out=x_sb[:], in_=x_rows[:, i * TILES : (i + 1) * TILES, :])
+            live["x", i] = x_sb
+
+        def statistics(i):
+            x_sb = live["x", i]
+            stats = small.tile([P, TILES, D // BN_MAX, 6], F32, name="stats")
+            mean_var = small.tile([P, TILES, 2], F32, name="mean_var")
+            for j in range(TILES):
+                for b in range(D // BN_MAX):
+                    nc.vector.bn_stats(out=stats[:, j, b, :], in_=x_sb[:, j, b * BN_MAX : (b + 1) * BN_MAX])
+                nc.vector.bn_aggr(out=mean_var[:, j, :], in_=stats[:, j, :, :].rearrange("p b s -> p (b s)"))
+            minus_mean = small.tile([P, TILES], F32, name="minus_mean")
+            nc.vector.tensor_scalar_mul(out=minus_mean[:], in0=mean_var[:, :, 0], scalar1=-1.0)
+            var_eps = small.tile([P, TILES], F32, name="var_eps")
+            nc.vector.tensor_scalar_add(out=var_eps[:], in0=mean_var[:, :, 1], scalar1=EPS)
+            live["minus_mean", i] = minus_mean
+            live["var_eps", i] = var_eps
+
+        def normalise(i):
+            x_sb = live["x", i]
+            minus_mean = live["minus_mean", i]
+            rstd = small.tile([P, TILES], F32, name="rstd")
+            nc.gpsimd.tensor_tensor(out=rstd[:], in0=live["var_eps", i][:], in1=minus_half[:], op=ALU.pow)
+            normed = work.tile([P, TILES, D], F32, name="normed")
+            for j in range(TILES):
+                nc.gpsimd.tensor_scalar(
+                    out=sorted_view(normed[:, j, :]),
+                    in0=feature_view(x_sb[:, j, :]),
+                    scalar1=minus_mean[:, j : j + 1],
+                    scalar2=rstd[:, j : j + 1],
+                    op0=ALU.add,
+                    op1=ALU.mult,
+                )
+            live["normed", i] = normed
+
+        def transpose_gain_shift(i):
+            normed = live["normed", i]
+            h_planes = work.tile([P, CHUNKS, GROUP_COLS], BF16, name="h_planes")
+            for c in range(CHUNKS):
+                normed_t = xt_psum.tile([P, TILES, P], F32, name="normed_t")
+                for j in range(TILES):
+                    nc.tensor.transpose(normed_t[:, j, :], normed[:, j, chunk_cols(c // PACK, c % PACK)], ident_f32[:])
+                nc.scalar.activation(
+                    out=h_planes[:, c, :],
+                    in_=normed_t[:].rearrange("p j r -> p (j r)"),
+                    func=ACT.Identity,
+                    scale=gain_shift[:, c : c + 1],
+                    bias=gain_shift[:, CHUNKS + c : CHUNKS + c + 1],
+                )
+            live["h_planes", i] = h_planes
+
+        def regroup(i):
+            h_planes = live["h_planes", i]
+            h_grouped = work.tile([P, PASSES, GROUP_COLS, PACK], BF16, name="h_grouped", align_bytes=64)
+            nc.vector.tensor_copy(
+                out=h_grouped[:, 0, :, :].rearrange("p (q s) t -> p q t s", s=4),
+                in_=h_planes[:, 0:PACK, :].rearrange("p t (q s) -> p q t s", s=4),
+            )
+            nc.scalar.copy(
+                out=h_grouped[:, 1, :, :].rearrange("p (q s) t -> p q t s", s=4),
+                in_=h_planes[:, PACK : 2 * PACK, :].rearrange("p t (q s) -> p q t s", s=4),
+            )
+            live["h_grouped", i] = h_grouped
+
+        def quantise(i):
+            h_grouped = live["h_grouped", i]
+            h_codes = work.tile([P, PASSES, GROUP_COLS], U32, name="h_codes", align_bytes=64)
+            h_scales = work.tile([P, PASSES, GROUP_COLS], U8, name="h_scales", align_bytes=64)
+            for g in range(PASSES):
+                nc.vector.quantize_mx(
+                    out=h_codes[:, g, :].bitcast(FP8X4),
+                    scales=h_scales[:, g, :],
+                    in_=h_grouped[:, g, :, :].rearrange("p r t -> p (r t)"),
+                )
+            live["h_codes", i] = h_codes
+            live["h_scales", i] = h_scales
+
+        def project(i):
+            h_codes = live["h_codes", i]
+            h_scales = live["h_scales", i]
+            fused = acc_psum.tile([P, TILES, W], F32, name="fused")
+            for j in range(TILES):
+                tile_cols = slice(j * P, (j + 1) * P)
+                for g in range(PASSES):
+                    nc.tensor.matmul_mx(
+                        out=fused[:, j, :],
+                        lhsT=h_codes[:, g, tile_cols].bitcast(FP8X4),
+                        lhsT_scale=h_scales[:, g, tile_cols],
+                        rhs=e_codes[:, g, :].bitcast(FP8X4),
+                        rhs_scale=e_scales[:, g, :],
+                        start=(g == 0),
+                        stop=(g == PASSES - 1),
+                    )
+            live["fused", i] = fused
+
+        def finish(i):
+            fused = live["fused", i]
+            results = out_pool.tile([P, 3, TILES, QK], F32, name="results")
+            nc.scalar.copy(
+                out=results[:, 0:2, :, :],
+                in_=fused[:, :, 0 : 2 * QK].rearrange("p j (w c) -> p w j c", w=2),
+            )
+            gelu = out_pool.tile([P, TILES, QK], F32, name="gelu")
+            nc.scalar.activation(out=gelu[:], in_=fused[:, :, 3 * QK : 4 * QK], func=ACT.Gelu)
+            nc.vector.tensor_tensor(
+                out=results[:, 2, :, :], in0=fused[:, :, 2 * QK : 3 * QK], in1=gelu[:], op=ALU.mult
+            )
+            for w in range(3):
+                nc.sync.dma_start(out=out_rows[w][:, i * TILES : (i + 1) * TILES, :], in_=results[:, w, :, :])
+
+        def run(stage, i):
+            if 0 <= i < GROUPS:
+                stage(i)
+
+        with tc.manual_schedule():
+            for i in range(X_BUFS - 1):
+                load(i)
+            for step in range(GROUPS + 4):
+                run(load, step + X_BUFS - 1)
+                run(statistics, step)
+                run(regroup, step - 2)
+                run(quantise, step - 2)
+                run(project, step - 3)
+                run(finish, step - 4)
+                run(normalise, step)
+                run(transpose_gain_shift, step - 1)

@@ -28,7 +28,7 @@ TILES = 4
 GROUP_COLS = TILES * P
 ROWS_PER_PARTITION = ROWS // P
 GROUPS = ROWS_PER_PARTITION // TILES
-X_BUFS = 4
+X_BUFS = 5
 STAGE_BUFS = 3
 
 FLOPS = 2 * ROWS * D * W
@@ -223,12 +223,12 @@ def tile_latentattentionblock_pa_t_kernel(tc, x, ln_gamma, ln_beta, expand, out_
         with tc.manual_schedule():
             for i in range(X_BUFS - 1):
                 load(i)
-            for step in range(GROUPS + 4):
+            for step in range(GROUPS + 5):
                 run(load, step + X_BUFS - 1)
                 run(statistics, step)
-                run(regroup, step - 2)
-                run(quantise, step - 2)
-                run(project, step - 3)
-                run(finish, step - 4)
-                run(normalise, step)
-                run(transpose_gain_shift, step - 1)
+                run(regroup, step - 3)
+                run(quantise, step - 3)
+                run(project, step - 4)
+                run(finish, step - 5)
+                run(normalise, step - 1)
+                run(transpose_gain_shift, step - 2)

@@ -28,6 +28,7 @@ TILES = 4
 GROUP_COLS = TILES * P
 ROWS_PER_PARTITION = ROWS // P
 GROUPS = ROWS_PER_PARTITION // TILES
+GATE_GROUPS = 5
 X_BUFS = 5
 STAGE_BUFS = 3
 
@@ -59,8 +60,6 @@ def tile_latentattentionblock_pa_t_kernel(tc, x, ln_gamma, ln_beta, expand, out_
         make_identity(nc, ident_f32[:])
         ident_bf16 = const.tile([P, P], BF16)
         make_identity(nc, ident_bf16[:])
-        minus_half = const.tile([P, TILES], F32)
-        nc.gpsimd.memset(minus_half[:], -0.5)
 
         vec_rows = const.tile([P, P], BF16)
         nc.vector.memset(vec_rows[:].bitcast(I32), 0)
@@ -109,34 +108,50 @@ def tile_latentattentionblock_pa_t_kernel(tc, x, ln_gamma, ln_beta, expand, out_
             nc.sync.dma_start(out=x_sb[:], in_=x_rows[:, i * TILES : (i + 1) * TILES, :])
             live["x", i] = x_sb
 
-        def statistics(i):
-            x_sb = live["x", i]
-            stats = small.tile([P, TILES, D // BN_MAX, 6], F32, name="stats")
-            mean_var = small.tile([P, TILES, 2], F32, name="mean_var")
-            for j in range(TILES):
-                for b in range(D // BN_MAX):
-                    nc.vector.bn_stats(out=stats[:, j, b, :], in_=x_sb[:, j, b * BN_MAX : (b + 1) * BN_MAX])
-                nc.vector.bn_aggr(out=mean_var[:, j, :], in_=stats[:, j, :, :].rearrange("p b s -> p (b s)"))
-            minus_mean = small.tile([P, TILES], F32, name="minus_mean")
-            nc.vector.tensor_scalar_mul(out=minus_mean[:], in0=mean_var[:, :, 0], scalar1=-1.0)
+        def tile_statistics(i, j):
+            for b in range(D // BN_MAX):
+                nc.vector.bn_stats(
+                    out=live["stats", i][:, j, b, :], in_=live["x", i][:, j, b * BN_MAX : (b + 1) * BN_MAX]
+                )
+            nc.vector.bn_aggr(
+                out=live["mean_var", i][:, j, :], in_=live["stats", i][:, j, :, :].rearrange("p b s -> p (b s)")
+            )
+
+        def statistics_first(i):
+            live["stats", i] = small.tile([P, TILES, D // BN_MAX, 6], F32, name="stats")
+            live["mean_var", i] = small.tile([P, TILES, 2], F32, name="mean_var")
+            tile_statistics(i, 0)
+
+        def statistics_rest(i):
+            for j in range(1, TILES):
+                tile_statistics(i, j)
             var_eps = small.tile([P, TILES], F32, name="var_eps")
-            nc.vector.tensor_scalar_add(out=var_eps[:], in0=mean_var[:, :, 1], scalar1=EPS)
-            live["minus_mean", i] = minus_mean
+            nc.vector.tensor_scalar_add(out=var_eps[:], in0=live["mean_var", i][:, :, 1], scalar1=EPS)
             live["var_eps", i] = var_eps
+
+        def deviation(i):
+            std = small.tile([P, TILES], F32, name="std")
+            nc.scalar.activation(out=std[:], in_=live["var_eps", i][:], func=ACT.Sqrt)
+            live["std", i] = std
+
+        def invert(i):
+            std = live["std", i]
+            rstd = small.tile([P, TILES], F32, name="rstd")
+            nc.vector.reciprocal(out=rstd[:], in_=std[:])
+            live["rstd", i] = rstd
 
         def normalise(i):
             x_sb = live["x", i]
-            minus_mean = live["minus_mean", i]
-            rstd = small.tile([P, TILES], F32, name="rstd")
-            nc.gpsimd.tensor_tensor(out=rstd[:], in0=live["var_eps", i][:], in1=minus_half[:], op=ALU.pow)
+            mean_var = live["mean_var", i]
+            rstd = live["rstd", i]
             normed = work.tile([P, TILES, D], F32, name="normed")
             for j in range(TILES):
                 nc.gpsimd.tensor_scalar(
                     out=sorted_view(normed[:, j, :]),
                     in0=feature_view(x_sb[:, j, :]),
-                    scalar1=minus_mean[:, j : j + 1],
+                    scalar1=mean_var[:, j, 0:1],
                     scalar2=rstd[:, j : j + 1],
-                    op0=ALU.add,
+                    op0=ALU.subtract,
                     op1=ALU.mult,
                 )
             live["normed", i] = normed
@@ -201,20 +216,26 @@ def tile_latentattentionblock_pa_t_kernel(tc, x, ln_gamma, ln_beta, expand, out_
                     )
             live["fused", i] = fused
 
+        gate_inputs = const.tile([P, 2, ROWS_PER_PARTITION, QK], F32)
+
         def finish(i):
             fused = live["fused", i]
-            results = out_pool.tile([P, 3, TILES, QK], F32, name="results")
+            rows = slice(i * TILES, (i + 1) * TILES)
+            results = out_pool.tile([P, 2, TILES, QK], F32, name="results")
+            nc.scalar.copy(out=results[:], in_=fused[:, :, 0 : 2 * QK].rearrange("p j (w c) -> p w j c", w=2))
             nc.scalar.copy(
-                out=results[:, 0:2, :, :],
-                in_=fused[:, :, 0 : 2 * QK].rearrange("p j (w c) -> p w j c", w=2),
+                out=gate_inputs[:, :, rows, :], in_=fused[:, :, 2 * QK : 4 * QK].rearrange("p j (w c) -> p w j c", w=2)
             )
-            gelu = out_pool.tile([P, TILES, QK], F32, name="gelu")
-            nc.scalar.activation(out=gelu[:], in_=fused[:, :, 3 * QK : 4 * QK], func=ACT.Gelu)
-            nc.vector.tensor_tensor(
-                out=results[:, 2, :, :], in0=fused[:, :, 2 * QK : 3 * QK], in1=gelu[:], op=ALU.mult
-            )
-            for w in range(3):
-                nc.sync.dma_start(out=out_rows[w][:, i * TILES : (i + 1) * TILES, :], in_=results[:, w, :, :])
+            for w in range(2):
+                nc.sync.dma_start(out=out_rows[w][:, rows, :], in_=results[:, w, :, :])
+
+        def gate(first, count):
+            rows = slice(first * TILES, (first + count) * TILES)
+            gelu = out_pool.tile([P, count * TILES, QK], F32, name="gelu%d" % count)
+            nc.scalar.activation(out=gelu[:], in_=gate_inputs[:, 1, rows, :], func=ACT.Gelu)
+            geglu = out_pool.tile([P, count * TILES, QK], F32, name="geglu%d" % count)
+            nc.vector.tensor_tensor(out=geglu[:], in0=gate_inputs[:, 0, rows, :], in1=gelu[:], op=ALU.mult)
+            nc.sync.dma_start(out=out_rows[2][:, rows, :], in_=geglu[:])
 
         def run(stage, i):
             if 0 <= i < GROUPS:
@@ -225,10 +246,17 @@ def tile_latentattentionblock_pa_t_kernel(tc, x, ln_gamma, ln_beta, expand, out_
                 load(i)
             for step in range(GROUPS + 5):
                 run(load, step + X_BUFS - 1)
-                run(statistics, step)
+                run(deviation, step - 1)
+                run(statistics_first, step)
+                run(invert, step - 1)
+                run(statistics_rest, step)
                 run(regroup, step - 3)
                 run(quantise, step - 3)
                 run(project, step - 4)
                 run(finish, step - 5)
                 run(normalise, step - 1)
                 run(transpose_gain_shift, step - 2)
+                if step == GROUPS + 3:
+                    for first in range(0, GROUPS - 1, GATE_GROUPS):
+                        gate(first, GATE_GROUPS)
+            gate(GROUPS - 1, 1)

@@ -127,7 +127,10 @@ def tile_latentattentionblock_pa_t_kernel(tc, x, ln_gamma, ln_beta, expand, out_
                 tile_statistics(i, j)
             var_eps = small.tile([P, TILES], F32, name="var_eps")
             nc.vector.tensor_scalar_add(out=var_eps[:], in0=live["mean_var", i][:, :, 1], scalar1=EPS)
+            minus_mean = small.tile([P, TILES], F32, name="minus_mean")
+            nc.vector.tensor_scalar_mul(out=minus_mean[:], in0=live["mean_var", i][:, :, 0], scalar1=-1.0)
             live["var_eps", i] = var_eps
+            live["minus_mean", i] = minus_mean
 
         def deviation(i):
             std = small.tile([P, TILES], F32, name="std")
@@ -142,16 +145,16 @@ def tile_latentattentionblock_pa_t_kernel(tc, x, ln_gamma, ln_beta, expand, out_
 
         def normalise(i):
             x_sb = live["x", i]
-            mean_var = live["mean_var", i]
+            minus_mean = live["minus_mean", i]
             rstd = live["rstd", i]
             normed = work.tile([P, TILES, D], F32, name="normed")
             for j in range(TILES):
                 nc.gpsimd.tensor_scalar(
                     out=sorted_view(normed[:, j, :]),
                     in0=feature_view(x_sb[:, j, :]),
-                    scalar1=mean_var[:, j, 0:1],
+                    scalar1=minus_mean[:, j : j + 1],
                     scalar2=rstd[:, j : j + 1],
-                    op0=ALU.subtract,
+                    op0=ALU.add,
                     op1=ALU.mult,
                 )
             live["normed", i] = normed

@@ -28,6 +28,7 @@ TILES = 4
 GROUP_COLS = TILES * P
 ROWS_PER_PARTITION = ROWS // P
 GROUPS = ROWS_PER_PARTITION // TILES
+SHARED_GROUPS = 2
 GATE_GROUPS = 5
 X_BUFS = 5
 STAGE_BUFS = 3
@@ -58,6 +59,8 @@ def tile_latentattentionblock_pa_t_kernel(tc, x, ln_gamma, ln_beta, expand, out_
 
         ident_f32 = const.tile([P, P], F32)
         make_identity(nc, ident_f32[:])
+        eps = const.tile([P, 1], F32)
+        nc.vector.memset(eps[:], EPS)
         ident_bf16 = const.tile([P, P], BF16)
         make_identity(nc, ident_bf16[:])
 
@@ -117,24 +120,18 @@ def tile_latentattentionblock_pa_t_kernel(tc, x, ln_gamma, ln_beta, expand, out_
                 out=live["mean_var", i][:, j, :], in_=live["stats", i][:, j, :, :].rearrange("p b s -> p (b s)")
             )
 
-        def statistics_first(i):
+        def statistics(i):
             live["stats", i] = small.tile([P, TILES, D // BN_MAX, 6], F32, name="stats")
             live["mean_var", i] = small.tile([P, TILES, 2], F32, name="mean_var")
-            tile_statistics(i, 0)
-
-        def statistics_rest(i):
-            for j in range(1, TILES):
+            for j in range(TILES):
                 tile_statistics(i, j)
-            var_eps = small.tile([P, TILES], F32, name="var_eps")
-            nc.vector.tensor_scalar_add(out=var_eps[:], in0=live["mean_var", i][:, :, 1], scalar1=EPS)
             minus_mean = small.tile([P, TILES], F32, name="minus_mean")
             nc.vector.tensor_scalar_mul(out=minus_mean[:], in0=live["mean_var", i][:, :, 0], scalar1=-1.0)
-            live["var_eps", i] = var_eps
             live["minus_mean", i] = minus_mean
 
         def deviation(i):
             std = small.tile([P, TILES], F32, name="std")
-            nc.scalar.activation(out=std[:], in_=live["var_eps", i][:], func=ACT.Sqrt)
+            nc.scalar.activation(out=std[:], in_=live["mean_var", i][:, :, 1], func=ACT.Sqrt, bias=eps[:])
             live["std", i] = std
 
         def invert(i):
@@ -149,7 +146,8 @@ def tile_latentattentionblock_pa_t_kernel(tc, x, ln_gamma, ln_beta, expand, out_
             rstd = live["rstd", i]
             normed = work.tile([P, TILES, D], F32, name="normed")
             for j in range(TILES):
-                nc.gpsimd.tensor_scalar(
+                engine = nc.vector if i == GROUPS - 1 and j % 2 else nc.gpsimd
+                engine.tensor_scalar(
                     out=sorted_view(normed[:, j, :]),
                     in0=feature_view(x_sb[:, j, :]),
                     scalar1=minus_mean[:, j : j + 1],
@@ -166,26 +164,29 @@ def tile_latentattentionblock_pa_t_kernel(tc, x, ln_gamma, ln_beta, expand, out_
                 normed_t = xt_psum.tile([P, TILES, P], F32, name="normed_t")
                 for j in range(TILES):
                     nc.tensor.transpose(normed_t[:, j, :], normed[:, j, chunk_cols(c // PACK, c % PACK)], ident_f32[:])
-                nc.scalar.activation(
-                    out=h_planes[:, c, :],
-                    in_=normed_t[:].rearrange("p j r -> p (j r)"),
-                    func=ACT.Identity,
-                    scale=gain_shift[:, c : c + 1],
-                    bias=gain_shift[:, CHUNKS + c : CHUNKS + c + 1],
-                )
+                gain = gain_shift[:, c : c + 1]
+                shift = gain_shift[:, CHUNKS + c : CHUNKS + c + 1]
+                source = normed_t[:].rearrange("p j r -> p (j r)")
+                if i >= GROUPS - SHARED_GROUPS and c % 2:
+                    nc.vector.tensor_scalar(
+                        out=h_planes[:, c, :], in0=source, scalar1=gain, scalar2=shift, op0=ALU.mult, op1=ALU.add
+                    )
+                else:
+                    nc.scalar.activation(out=h_planes[:, c, :], in_=source, func=ACT.Identity, scale=gain, bias=shift)
             live["h_planes", i] = h_planes
 
         def regroup(i):
             h_planes = live["h_planes", i]
             h_grouped = work.tile([P, PASSES, GROUP_COLS, PACK], BF16, name="h_grouped", align_bytes=64)
-            nc.vector.tensor_copy(
-                out=h_grouped[:, 0, :, :].rearrange("p (q s) t -> p q t s", s=4),
-                in_=h_planes[:, 0:PACK, :].rearrange("p t (q s) -> p q t s", s=4),
-            )
-            nc.scalar.copy(
-                out=h_grouped[:, 1, :, :].rearrange("p (q s) t -> p q t s", s=4),
-                in_=h_planes[:, PACK : 2 * PACK, :].rearrange("p t (q s) -> p q t s", s=4),
-            )
+            for copy, g, cols in (
+                (nc.scalar.copy, 1, slice(P, GROUP_COLS)),
+                (nc.vector.tensor_copy, 0, slice(0, GROUP_COLS)),
+                (nc.vector.tensor_copy, 1, slice(0, P)),
+            ):
+                copy(
+                    out=h_grouped[:, g, cols, :].rearrange("p (q s) t -> p q t s", s=4),
+                    in_=h_planes[:, g * PACK : (g + 1) * PACK, cols].rearrange("p t (q s) -> p q t s", s=4),
+                )
             live["h_grouped", i] = h_grouped
 
         def quantise(i):
@@ -250,15 +251,14 @@ def tile_latentattentionblock_pa_t_kernel(tc, x, ln_gamma, ln_beta, expand, out_
             for step in range(GROUPS + 5):
                 run(load, step + X_BUFS - 1)
                 run(deviation, step - 1)
-                run(statistics_first, step)
                 run(invert, step - 1)
-                run(statistics_rest, step)
+                run(statistics, step)
                 run(regroup, step - 3)
                 run(quantise, step - 3)
-                run(project, step - 4)
-                run(finish, step - 5)
                 run(normalise, step - 1)
                 run(transpose_gain_shift, step - 2)
+                run(project, step - 4)
+                run(finish, step - 5)
                 if step == GROUPS + 3:
                     for first in range(0, GROUPS - 1, GATE_GROUPS):
                         gate(first, GATE_GROUPS)

@@ -111,23 +111,17 @@ def tile_latentattentionblock_pa_t_kernel(tc, x, ln_gamma, ln_beta, expand, out_
             nc.sync.dma_start(out=x_sb[:], in_=x_rows[:, i * TILES : (i + 1) * TILES, :])
             live["x", i] = x_sb
 
-        def tile_statistics(i, j):
-            for b in range(D // BN_MAX):
-                nc.vector.bn_stats(
-                    out=live["stats", i][:, j, b, :], in_=live["x", i][:, j, b * BN_MAX : (b + 1) * BN_MAX]
-                )
-            nc.vector.bn_aggr(
-                out=live["mean_var", i][:, j, :], in_=live["stats", i][:, j, :, :].rearrange("p b s -> p (b s)")
-            )
-
         def statistics(i):
-            live["stats", i] = small.tile([P, TILES, D // BN_MAX, 6], F32, name="stats")
-            live["mean_var", i] = small.tile([P, TILES, 2], F32, name="mean_var")
+            stats = small.tile([P, TILES, D // BN_MAX, 6], F32, name="stats")
+            mean_var = small.tile([P, TILES, 2], F32, name="mean_var")
             for j in range(TILES):
-                tile_statistics(i, j)
-            minus_mean = small.tile([P, TILES], F32, name="minus_mean")
-            nc.vector.tensor_scalar_mul(out=minus_mean[:], in0=live["mean_var", i][:, :, 0], scalar1=-1.0)
-            live["minus_mean", i] = minus_mean
+                for b in range(D // BN_MAX):
+                    nc.vector.bn_stats(
+                        out=stats[:, j, b, :], in_=live["x", i][:, j, b * BN_MAX : (b + 1) * BN_MAX]
+                    )
+            for j in range(TILES):
+                nc.vector.bn_aggr(out=mean_var[:, j, :], in_=stats[:, j, :, :].rearrange("p b s -> p (b s)"))
+            live["mean_var", i] = mean_var
 
         def deviation(i):
             std = small.tile([P, TILES], F32, name="std")
@@ -138,7 +132,10 @@ def tile_latentattentionblock_pa_t_kernel(tc, x, ln_gamma, ln_beta, expand, out_
             std = live["std", i]
             rstd = small.tile([P, TILES], F32, name="rstd")
             nc.vector.reciprocal(out=rstd[:], in_=std[:])
+            minus_mean = small.tile([P, TILES], F32, name="minus_mean")
+            nc.vector.tensor_scalar_mul(out=minus_mean[:], in0=live["mean_var", i][:, :, 0], scalar1=-1.0)
             live["rstd", i] = rstd
+            live["minus_mean", i] = minus_mean
 
         def normalise(i):
             x_sb = live["x", i]
@@ -193,12 +190,11 @@ def tile_latentattentionblock_pa_t_kernel(tc, x, ln_gamma, ln_beta, expand, out_
             h_grouped = live["h_grouped", i]
             h_codes = work.tile([P, PASSES, GROUP_COLS], U32, name="h_codes", align_bytes=64)
             h_scales = work.tile([P, PASSES, GROUP_COLS], U8, name="h_scales", align_bytes=64)
-            for g in range(PASSES):
-                nc.vector.quantize_mx(
-                    out=h_codes[:, g, :].bitcast(FP8X4),
-                    scales=h_scales[:, g, :],
-                    in_=h_grouped[:, g, :, :].rearrange("p r t -> p (r t)"),
-                )
+            nc.vector.quantize_mx(
+                out=h_codes[:].rearrange("p g r -> p (g r)").bitcast(FP8X4),
+                scales=h_scales[:].rearrange("p g r -> p (g r)"),
+                in_=h_grouped[:].rearrange("p g r t -> p (g r t)"),
+            )
             live["h_codes", i] = h_codes
             live["h_scales", i] = h_scales
 
@@ -248,18 +244,18 @@ def tile_latentattentionblock_pa_t_kernel(tc, x, ln_gamma, ln_beta, expand, out_
         with tc.manual_schedule():
             for i in range(X_BUFS - 1):
                 load(i)
-            for step in range(GROUPS + 5):
+            for step in range(GROUPS + 6):
                 run(load, step + X_BUFS - 1)
                 run(deviation, step - 1)
                 run(invert, step - 1)
                 run(statistics, step)
+                run(quantise, step - 4)
                 run(regroup, step - 3)
-                run(quantise, step - 3)
                 run(normalise, step - 1)
                 run(transpose_gain_shift, step - 2)
-                run(project, step - 4)
-                run(finish, step - 5)
-                if step == GROUPS + 3:
+                run(project, step - 5)
+                run(finish, step - 6)
+                if step == GROUPS + 4:
                     for first in range(0, GROUPS - 1, GATE_GROUPS):
                         gate(first, GATE_GROUPS)
             gate(GROUPS - 1, 1)

@@ -175,14 +175,10 @@ def tile_latentattentionblock_pa_t_kernel(tc, x, ln_gamma, ln_beta, expand, out_
         def regroup(i):
             h_planes = live["h_planes", i]
             h_grouped = work.tile([P, PASSES, GROUP_COLS, PACK], BF16, name="h_grouped", align_bytes=64)
-            for copy, g, cols in (
-                (nc.scalar.copy, 1, slice(P, GROUP_COLS)),
-                (nc.vector.tensor_copy, 0, slice(0, GROUP_COLS)),
-                (nc.vector.tensor_copy, 1, slice(0, P)),
-            ):
+            for g, copy in enumerate((nc.vector.tensor_copy, nc.scalar.copy)):
                 copy(
-                    out=h_grouped[:, g, cols, :].rearrange("p (q s) t -> p q t s", s=4),
-                    in_=h_planes[:, g * PACK : (g + 1) * PACK, cols].rearrange("p t (q s) -> p q t s", s=4),
+                    out=h_grouped[:, g, :, :].rearrange("p (q s) t -> p q t s", s=4),
+                    in_=h_planes[:, g * PACK : (g + 1) * PACK, :].rearrange("p t (q s) -> p q t s", s=4),
                 )
             live["h_grouped", i] = h_grouped
 

@@ -16,6 +16,7 @@ P = 128
 ROWS = 16 * 512
 D = 1024
 W = 128
+PARTS = 4
 QK = 32
 EPS = 1e-5
 PACK = 4
@@ -24,12 +25,12 @@ K_PASS = P * PACK
 PASSES = D // K_PASS
 CHUNKS = D // P
 BN_MAX = 512
+TILE_COUNT = ROWS // P
 TILES = 4
-GROUP_COLS = TILES * P
-ROWS_PER_PARTITION = ROWS // P
-GROUPS = ROWS_PER_PARTITION // TILES
+GROUP_TILES = (2,) + (TILES,) * ((TILE_COUNT - 4) // TILES) + (2,)
+GROUPS = len(GROUP_TILES)
 SHARED_GROUPS = 2
-GATE_GROUPS = 5
+EARLY_GATES = GROUPS - 2
 X_BUFS = 5
 STAGE_BUFS = 3
 
@@ -56,38 +57,61 @@ def tile_latentattentionblock_pa_t_kernel(tc, x, ln_gamma, ln_beta, expand, out_
 
     with ExitStack() as stack:
         const = stack.enter_context(tc.tile_pool(name="const", bufs=1))
+        x_pool = stack.enter_context(tc.tile_pool(name="x_pool", bufs=X_BUFS))
+        small = stack.enter_context(tc.tile_pool(name="small", bufs=STAGE_BUFS))
+        work = stack.enter_context(tc.tile_pool(name="work", bufs=STAGE_BUFS))
+        gate_pool = stack.enter_context(tc.tile_pool(name="gate_pool", bufs=3))
+        xt_psum = stack.enter_context(tc.psum_pool(name="xt_psum", bufs=6))
+        acc_psum = stack.enter_context(tc.psum_pool(name="acc_psum", bufs=2))
 
         ident_f32 = const.tile([P, P], F32)
-        make_identity(nc, ident_f32[:])
-        eps = const.tile([P, 1], F32)
-        nc.vector.memset(eps[:], EPS)
         ident_bf16 = const.tile([P, P], BF16)
-        make_identity(nc, ident_bf16[:])
-
+        eps = const.tile([P, 1], F32)
         vec_rows = const.tile([P, P], BF16)
-        nc.vector.memset(vec_rows[:].bitcast(I32), 0)
-        for v, vec in enumerate((ln_gamma, ln_beta)):
-            vec_view = vec.rearrange("(g b t r) -> g t b r", g=PASSES, t=PACK, r=RUN)
-            for g in range(PASSES):
-                row = v * CHUNKS + g * PACK
-                nc.scalar.dma_start(
-                    out=vec_rows[row : row + PACK, :].rearrange("t (b r) -> t b r", r=RUN), in_=vec_view[g]
-                )
-        expand_sb = const.tile([W, D], BF16)
-        nc.scalar.dma_start(out=expand_sb[:], in_=expand)
-        expand_sorted = const.tile([W, D], BF16)
-        nc.vector.tensor_copy(out=sorted_view(expand_sorted[:]), in_=feature_view(expand_sb[:]))
-
         gain_shift = const.tile([P, 2 * CHUNKS], F32)
+        expand_sb = const.tile([W, D], BF16)
+        expand_sorted = const.tile([W, D], BF16)
         e_grouped = const.tile([P, PASSES, W, PACK], BF16, align_bytes=64)
         e_codes = const.tile([P, PASSES, W], U32, align_bytes=64)
         e_scales = const.tile([P, PASSES, W], U8, align_bytes=64)
-        with tc.psum_pool(name="setup_psum", bufs=1) as setup_psum:
-            vec_cols = setup_psum.tile([P, P], BF16)
+        parts = const.tile([P, PARTS, TILE_COUNT, QK], F32)
+
+        live = {}
+
+        def tiles_of(i):
+            first = sum(GROUP_TILES[:i])
+            return slice(first, first + GROUP_TILES[i])
+
+        def load(i):
+            x_sb = x_pool.tile([P, GROUP_TILES[i], D], BF16, name="x_sb")
+            nc.sync.dma_start(out=x_sb[:], in_=x_rows[:, tiles_of(i), :])
+            live["x", i] = x_sb
+
+        def load_constants():
+            make_identity(nc, ident_f32[:])
+            make_identity(nc, ident_bf16[:])
+            nc.vector.memset(eps[:], EPS)
+            nc.vector.memset(vec_rows[:].bitcast(I32), 0)
+            for v, vec in enumerate((ln_gamma, ln_beta)):
+                vec_view = vec.rearrange("(g b t r) -> g t b r", g=PASSES, t=PACK, r=RUN)
+                for g in range(PASSES):
+                    row = v * CHUNKS + g * PACK
+                    nc.scalar.dma_start(
+                        out=vec_rows[row : row + PACK, :].rearrange("t (b r) -> t b r", r=RUN), in_=vec_view[g]
+                    )
+            nc.scalar.dma_start(out=expand_sb[:], in_=expand)
+
+        def prepare_gain_shift():
+            vec_cols = xt_psum.tile([P, P], BF16, name="normed_t")
             nc.tensor.transpose(vec_cols[:], vec_rows[:], ident_bf16[:])
             nc.vector.tensor_copy(out=gain_shift[:], in_=vec_cols[:, 0 : 2 * CHUNKS])
+
+        def sort_expand():
+            nc.vector.tensor_copy(out=sorted_view(expand_sorted[:]), in_=feature_view(expand_sb[:]))
+
+        def prepare_expand():
             for g in range(PASSES):
-                e_t = setup_psum.tile([P, PACK, W], BF16, name="e_t%d" % g)
+                e_t = xt_psum.tile([P, PACK, W], BF16, name="normed_t")
                 for t in range(PACK):
                     nc.tensor.transpose(e_t[:, t, :], expand_sorted[:, chunk_cols(g, t)], ident_bf16[:])
                 nc.vector.tensor_copy(out=e_grouped[:, g, :, :], in_=e_t[:].rearrange("p t o -> p o t"))
@@ -97,69 +121,54 @@ def tile_latentattentionblock_pa_t_kernel(tc, x, ln_gamma, ln_beta, expand, out_
                 in_=e_grouped[:].rearrange("p g o t -> p (g o t)"),
             )
 
-        x_pool = stack.enter_context(tc.tile_pool(name="x_pool", bufs=X_BUFS))
-        small = stack.enter_context(tc.tile_pool(name="small", bufs=STAGE_BUFS))
-        work = stack.enter_context(tc.tile_pool(name="work", bufs=STAGE_BUFS))
-        out_pool = stack.enter_context(tc.tile_pool(name="out_pool", bufs=STAGE_BUFS))
-        xt_psum = stack.enter_context(tc.psum_pool(name="xt_psum", bufs=6))
-        acc_psum = stack.enter_context(tc.psum_pool(name="acc_psum", bufs=2))
-
-        live = {}
-
-        def load(i):
-            x_sb = x_pool.tile([P, TILES, D], BF16, name="x_sb")
-            nc.sync.dma_start(out=x_sb[:], in_=x_rows[:, i * TILES : (i + 1) * TILES, :])
-            live["x", i] = x_sb
-
         def statistics(i):
-            stats = small.tile([P, TILES, D // BN_MAX, 6], F32, name="stats")
-            mean_var = small.tile([P, TILES, 2], F32, name="mean_var")
-            for j in range(TILES):
+            n = GROUP_TILES[i]
+            stats = small.tile([P, n, D // BN_MAX, 6], F32, name="stats")
+            mean_var = small.tile([P, n, 2], F32, name="mean_var")
+            for j in range(n):
                 for b in range(D // BN_MAX):
                     nc.vector.bn_stats(
                         out=stats[:, j, b, :], in_=live["x", i][:, j, b * BN_MAX : (b + 1) * BN_MAX]
                     )
-            for j in range(TILES):
+            for j in range(n):
                 nc.vector.bn_aggr(out=mean_var[:, j, :], in_=stats[:, j, :, :].rearrange("p b s -> p (b s)"))
             live["mean_var", i] = mean_var
 
         def deviation(i):
-            std = small.tile([P, TILES], F32, name="std")
+            std = small.tile([P, GROUP_TILES[i]], F32, name="std")
             nc.scalar.activation(out=std[:], in_=live["mean_var", i][:, :, 1], func=ACT.Sqrt, bias=eps[:])
             live["std", i] = std
 
         def invert(i):
-            std = live["std", i]
-            rstd = small.tile([P, TILES], F32, name="rstd")
-            nc.vector.reciprocal(out=rstd[:], in_=std[:])
-            minus_mean = small.tile([P, TILES], F32, name="minus_mean")
+            rstd = small.tile([P, GROUP_TILES[i]], F32, name="rstd")
+            nc.vector.reciprocal(out=rstd[:], in_=live["std", i][:])
+            minus_mean = small.tile([P, GROUP_TILES[i]], F32, name="minus_mean")
             nc.vector.tensor_scalar_mul(out=minus_mean[:], in0=live["mean_var", i][:, :, 0], scalar1=-1.0)
             live["rstd", i] = rstd
             live["minus_mean", i] = minus_mean
 
         def normalise(i):
-            x_sb = live["x", i]
-            minus_mean = live["minus_mean", i]
-            rstd = live["rstd", i]
-            normed = work.tile([P, TILES, D], F32, name="normed")
-            for j in range(TILES):
+            n = GROUP_TILES[i]
+            normed = work.tile([P, n, D], F32, name="normed")
+            for j in range(n):
                 engine = nc.vector if i == GROUPS - 1 and j % 2 else nc.gpsimd
                 engine.tensor_scalar(
                     out=sorted_view(normed[:, j, :]),
-                    in0=feature_view(x_sb[:, j, :]),
-                    scalar1=minus_mean[:, j : j + 1],
-                    scalar2=rstd[:, j : j + 1],
+                    in0=feature_view(live["x", i][:, j, :]),
+                    scalar1=live["minus_mean", i][:, j : j + 1],
+                    scalar2=live["rstd", i][:, j : j + 1],
                     op0=ALU.add,
                     op1=ALU.mult,
                 )
             live["normed", i] = normed
 
         def transpose_gain_shift(i):
+            n = GROUP_TILES[i]
             normed = live["normed", i]
-            h_planes = work.tile([P, CHUNKS, GROUP_COLS], BF16, name="h_planes")
+            h_planes = work.tile([P, CHUNKS, n * P], BF16, name="h_planes")
             for c in range(CHUNKS):
-                normed_t = xt_psum.tile([P, TILES, P], F32, name="normed_t")
-                for j in range(TILES):
+                normed_t = xt_psum.tile([P, n, P], F32, name="normed_t")
+                for j in range(n):
                     nc.tensor.transpose(normed_t[:, j, :], normed[:, j, chunk_cols(c // PACK, c % PACK)], ident_f32[:])
                 gain = gain_shift[:, c : c + 1]
                 shift = gain_shift[:, CHUNKS + c : CHUNKS + c + 1]
@@ -174,7 +183,7 @@ def tile_latentattentionblock_pa_t_kernel(tc, x, ln_gamma, ln_beta, expand, out_
 
         def regroup(i):
             h_planes = live["h_planes", i]
-            h_grouped = work.tile([P, PASSES, GROUP_COLS, PACK], BF16, name="h_grouped", align_bytes=64)
+            h_grouped = work.tile([P, PASSES, GROUP_TILES[i] * P, PACK], BF16, name="h_grouped", align_bytes=64)
             for g, copy in enumerate((nc.vector.tensor_copy, nc.scalar.copy)):
                 copy(
                     out=h_grouped[:, g, :, :].rearrange("p (q s) t -> p q t s", s=4),
@@ -183,13 +192,13 @@ def tile_latentattentionblock_pa_t_kernel(tc, x, ln_gamma, ln_beta, expand, out_
             live["h_grouped", i] = h_grouped
 
         def quantise(i):
-            h_grouped = live["h_grouped", i]
-            h_codes = work.tile([P, PASSES, GROUP_COLS], U32, name="h_codes", align_bytes=64)
-            h_scales = work.tile([P, PASSES, GROUP_COLS], U8, name="h_scales", align_bytes=64)
+            cols = GROUP_TILES[i] * P
+            h_codes = work.tile([P, PASSES, cols], U32, name="h_codes", align_bytes=64)
+            h_scales = work.tile([P, PASSES, cols], U8, name="h_scales", align_bytes=64)
             nc.vector.quantize_mx(
                 out=h_codes[:].rearrange("p g r -> p (g r)").bitcast(FP8X4),
                 scales=h_scales[:].rearrange("p g r -> p (g r)"),
-                in_=h_grouped[:].rearrange("p g r t -> p (g r t)"),
+                in_=live["h_grouped", i][:].rearrange("p g r t -> p (g r t)"),
             )
             live["h_codes", i] = h_codes
             live["h_scales", i] = h_scales
@@ -197,8 +206,8 @@ def tile_latentattentionblock_pa_t_kernel(tc, x, ln_gamma, ln_beta, expand, out_
         def project(i):
             h_codes = live["h_codes", i]
             h_scales = live["h_scales", i]
-            fused = acc_psum.tile([P, TILES, W], F32, name="fused")
-            for j in range(TILES):
+            fused = acc_psum.tile([P, GROUP_TILES[i], W], F32, name="fused")
+            for j in range(GROUP_TILES[i]):
                 tile_cols = slice(j * P, (j + 1) * P)
                 for g in range(PASSES):
                     nc.tensor.matmul_mx(
@@ -212,25 +221,20 @@ def tile_latentattentionblock_pa_t_kernel(tc, x, ln_gamma, ln_beta, expand, out_
                     )
             live["fused", i] = fused
 
-        gate_inputs = const.tile([P, 2, ROWS_PER_PARTITION, QK], F32)
-
         def finish(i):
-            fused = live["fused", i]
-            rows = slice(i * TILES, (i + 1) * TILES)
-            results = out_pool.tile([P, 2, TILES, QK], F32, name="results")
-            nc.scalar.copy(out=results[:], in_=fused[:, :, 0 : 2 * QK].rearrange("p j (w c) -> p w j c", w=2))
+            rows = tiles_of(i)
             nc.scalar.copy(
-                out=gate_inputs[:, :, rows, :], in_=fused[:, :, 2 * QK : 4 * QK].rearrange("p j (w c) -> p w j c", w=2)
+                out=parts[:, :, rows, :], in_=live["fused", i][:].rearrange("p j (w c) -> p w j c", w=PARTS)
             )
             for w in range(2):
-                nc.sync.dma_start(out=out_rows[w][:, rows, :], in_=results[:, w, :, :])
+                nc.sync.dma_start(out=out_rows[w][:, rows, :], in_=parts[:, w, rows, :])
 
-        def gate(first, count):
-            rows = slice(first * TILES, (first + count) * TILES)
-            gelu = out_pool.tile([P, count * TILES, QK], F32, name="gelu%d" % count)
-            nc.scalar.activation(out=gelu[:], in_=gate_inputs[:, 1, rows, :], func=ACT.Gelu)
-            geglu = out_pool.tile([P, count * TILES, QK], F32, name="geglu%d" % count)
-            nc.vector.tensor_tensor(out=geglu[:], in0=gate_inputs[:, 0, rows, :], in1=gelu[:], op=ALU.mult)
+        def gate(first, last):
+            rows = slice(tiles_of(first).start, tiles_of(last - 1).stop)
+            gelu = gate_pool.tile([P, rows.stop - rows.start, QK], F32, name="gelu")
+            nc.scalar.activation(out=gelu[:], in_=parts[:, 3, rows, :], func=ACT.Gelu)
+            geglu = gate_pool.tile([P, rows.stop - rows.start, QK], F32, name="geglu")
+            nc.vector.tensor_tensor(out=geglu[:], in0=parts[:, 2, rows, :], in1=gelu[:], op=ALU.mult)
             nc.sync.dma_start(out=out_rows[2][:, rows, :], in_=geglu[:])
 
         def run(stage, i):
@@ -240,18 +244,24 @@ def tile_latentattentionblock_pa_t_kernel(tc, x, ln_gamma, ln_beta, expand, out_
         with tc.manual_schedule():
             for i in range(X_BUFS - 1):
                 load(i)
+            load_constants()
             for step in range(GROUPS + 6):
                 run(load, step + X_BUFS - 1)
-                run(deviation, step - 1)
                 run(invert, step - 1)
                 run(statistics, step)
+                if step == 1:
+                    prepare_gain_shift()
+                    sort_expand()
                 run(quantise, step - 4)
                 run(regroup, step - 3)
                 run(normalise, step - 1)
                 run(transpose_gain_shift, step - 2)
+                run(deviation, step)
+                if step == 2:
+                    prepare_expand()
                 run(project, step - 5)
                 run(finish, step - 6)
-                if step == GROUPS + 4:
-                    for first in range(0, GROUPS - 1, GATE_GROUPS):
-                        gate(first, GATE_GROUPS)
-            gate(GROUPS - 1, 1)
+                if step == GROUPS + 3:
+                    gate(0, EARLY_GATES // 2)
+                    gate(EARLY_GATES // 2, EARLY_GATES)
+            gate(EARLY_GATES, GROUPS)

@@ -31,6 +31,7 @@ GROUP_TILES = (2,) + (TILES,) * ((TILE_COUNT - 4) // TILES) + (2,)
 GROUPS = len(GROUP_TILES)
 SHARED_GROUPS = 2
 EARLY_GATES = GROUPS - 2
+VECTOR_TILES = 3
 X_BUFS = 5
 STAGE_BUFS = 3
 
@@ -182,13 +183,20 @@ def tile_latentattentionblock_pa_t_kernel(tc, x, ln_gamma, ln_beta, expand, out_
             live["h_planes", i] = h_planes
 
         def regroup(i):
+            cols = GROUP_TILES[i] * P
+            vector_cols = min(cols, VECTOR_TILES * P)
             h_planes = live["h_planes", i]
-            h_grouped = work.tile([P, PASSES, GROUP_TILES[i] * P, PACK], BF16, name="h_grouped", align_bytes=64)
-            for g, copy in enumerate((nc.vector.tensor_copy, nc.scalar.copy)):
-                copy(
-                    out=h_grouped[:, g, :, :].rearrange("p (q s) t -> p q t s", s=4),
-                    in_=h_planes[:, g * PACK : (g + 1) * PACK, :].rearrange("p t (q s) -> p q t s", s=4),
-                )
+            h_grouped = work.tile([P, PASSES, cols, PACK], BF16, name="h_grouped", align_bytes=64)
+            for copy, g, part in (
+                (nc.vector.tensor_copy, 0, slice(0, vector_cols)),
+                (nc.scalar.copy, 0, slice(vector_cols, cols)),
+                (nc.scalar.copy, 1, slice(0, cols)),
+            ):
+                if part.start < part.stop:
+                    copy(
+                        out=h_grouped[:, g, part, :].rearrange("p (q s) t -> p q t s", s=4),
+                        in_=h_planes[:, g * PACK : (g + 1) * PACK, part].rearrange("p t (q s) -> p q t s", s=4),
+                    )
             live["h_grouped", i] = h_grouped
 
         def quantise(i):

from contextlib import ExitStack

import concourse.mybir as mybir
from concourse.masks import make_identity

F32 = mybir.dt.float32
BF16 = mybir.dt.bfloat16
U32 = mybir.dt.uint32
U8 = mybir.dt.uint8
I32 = mybir.dt.int32
FP8X4 = mybir.dt.float8_e4m3fn_x4
ALU = mybir.AluOpType
ACT = mybir.ActivationFunctionType

P = 128
ROWS = 16 * 512
D = 1024
W = 128
PARTS = 4
QK = 32
EPS = 1e-5
PACK = 4
RUN = 8
K_PASS = P * PACK
PASSES = D // K_PASS
CHUNKS = D // P
BN_MAX = 512
TILE_COUNT = ROWS // P
TILES = 4
GROUP_TILES = (2,) + (TILES,) * ((TILE_COUNT - 4) // TILES) + (2,)
GROUPS = len(GROUP_TILES)
SHARED_GROUPS = 2
EARLY_GATES = GROUPS - 2
VECTOR_TILES = 3
X_BUFS = 5
STAGE_BUFS = 3

FLOPS = 2 * ROWS * D * W


def feature_view(row):
    return row.rearrange("p (q t r) -> p t q r", t=PACK, r=RUN)


def sorted_view(row):
    return row.rearrange("p (t q r) -> p t q r", t=PACK, r=RUN)


def chunk_cols(g, t):
    first = t * (D // PACK) + g * P
    return slice(first, first + P)


def tile_latentattentionblock_pa_t_kernel(tc, x, ln_gamma, ln_beta, expand, out_0, out_1, out_2):
    nc = tc.nc
    x_rows = x.flatten_outer_dims().rearrange("(p j) d -> p j d", p=P)
    out_rows = [o.flatten_outer_dims().rearrange("(p j) c -> p j c", p=P) for o in (out_0, out_1, out_2)]

    with ExitStack() as stack:
        const = stack.enter_context(tc.tile_pool(name="const", bufs=1))
        x_pool = stack.enter_context(tc.tile_pool(name="x_pool", bufs=X_BUFS))
        small = stack.enter_context(tc.tile_pool(name="small", bufs=STAGE_BUFS))
        work = stack.enter_context(tc.tile_pool(name="work", bufs=STAGE_BUFS))
        gate_pool = stack.enter_context(tc.tile_pool(name="gate_pool", bufs=3))
        xt_psum = stack.enter_context(tc.psum_pool(name="xt_psum", bufs=6))
        acc_psum = stack.enter_context(tc.psum_pool(name="acc_psum", bufs=2))

        ident_f32 = const.tile([P, P], F32)
        ident_bf16 = const.tile([P, P], BF16)
        eps = const.tile([P, 1], F32)
        vec_rows = const.tile([P, P], BF16)
        gain_shift = const.tile([P, 2 * CHUNKS], F32)
        expand_sb = const.tile([W, D], BF16)
        expand_sorted = const.tile([W, D], BF16)
        e_grouped = const.tile([P, PASSES, W, PACK], BF16, align_bytes=64)
        e_codes = const.tile([P, PASSES, W], U32, align_bytes=64)
        e_scales = const.tile([P, PASSES, W], U8, align_bytes=64)
        parts = const.tile([P, PARTS, TILE_COUNT, QK], F32)

        live = {}

        def tiles_of(i):
            first = sum(GROUP_TILES[:i])
            return slice(first, first + GROUP_TILES[i])

        def load(i):
            x_sb = x_pool.tile([P, GROUP_TILES[i], D], BF16, name="x_sb")
            nc.sync.dma_start(out=x_sb[:], in_=x_rows[:, tiles_of(i), :])
            live["x", i] = x_sb

        def load_constants():
            make_identity(nc, ident_f32[:])
            make_identity(nc, ident_bf16[:])
            nc.vector.memset(eps[:], EPS)
            nc.vector.memset(vec_rows[:].bitcast(I32), 0)
            for v, vec in enumerate((ln_gamma, ln_beta)):
                vec_view = vec.rearrange("(g b t r) -> g t b r", g=PASSES, t=PACK, r=RUN)
                for g in range(PASSES):
                    row = v * CHUNKS + g * PACK
                    nc.scalar.dma_start(
                        out=vec_rows[row : row + PACK, :].rearrange("t (b r) -> t b r", r=RUN), in_=vec_view[g]
                    )
            nc.scalar.dma_start(out=expand_sb[:], in_=expand)

        def prepare_gain_shift():
            vec_cols = xt_psum.tile([P, P], BF16, name="normed_t")
            nc.tensor.transpose(vec_cols[:], vec_rows[:], ident_bf16[:])
            nc.vector.tensor_copy(out=gain_shift[:], in_=vec_cols[:, 0 : 2 * CHUNKS])

        def sort_expand():
            nc.vector.tensor_copy(out=sorted_view(expand_sorted[:]), in_=feature_view(expand_sb[:]))

        def prepare_expand():
            for g in range(PASSES):
                e_t = xt_psum.tile([P, PACK, W], BF16, name="normed_t")
                for t in range(PACK):
                    nc.tensor.transpose(e_t[:, t, :], expand_sorted[:, chunk_cols(g, t)], ident_bf16[:])
                nc.vector.tensor_copy(out=e_grouped[:, g, :, :], in_=e_t[:].rearrange("p t o -> p o t"))
            nc.vector.quantize_mx(
                out=e_codes[:].rearrange("p g o -> p (g o)").bitcast(FP8X4),
                scales=e_scales[:].rearrange("p g o -> p (g o)"),
                in_=e_grouped[:].rearrange("p g o t -> p (g o t)"),
            )

        def statistics(i):
            n = GROUP_TILES[i]
            stats = small.tile([P, n, D // BN_MAX, 6], F32, name="stats")
            mean_var = small.tile([P, n, 2], F32, name="mean_var")
            for j in range(n):
                for b in range(D // BN_MAX):
                    nc.vector.bn_stats(
                        out=stats[:, j, b, :], in_=live["x", i][:, j, b * BN_MAX : (b + 1) * BN_MAX]
                    )
            for j in range(n):
                nc.vector.bn_aggr(out=mean_var[:, j, :], in_=stats[:, j, :, :].rearrange("p b s -> p (b s)"))
            live["mean_var", i] = mean_var

        def deviation(i):
            std = small.tile([P, GROUP_TILES[i]], F32, name="std")
            nc.scalar.activation(out=std[:], in_=live["mean_var", i][:, :, 1], func=ACT.Sqrt, bias=eps[:])
            live["std", i] = std

        def invert(i):
            rstd = small.tile([P, GROUP_TILES[i]], F32, name="rstd")
            nc.vector.reciprocal(out=rstd[:], in_=live["std", i][:])
            minus_mean = small.tile([P, GROUP_TILES[i]], F32, name="minus_mean")
            nc.vector.tensor_scalar_mul(out=minus_mean[:], in0=live["mean_var", i][:, :, 0], scalar1=-1.0)
            live["rstd", i] = rstd
            live["minus_mean", i] = minus_mean

        def normalise(i):
            n = GROUP_TILES[i]
            normed = work.tile([P, n, D], F32, name="normed")
            for j in range(n):
                engine = nc.vector if i == GROUPS - 1 and j % 2 else nc.gpsimd
                engine.tensor_scalar(
                    out=sorted_view(normed[:, j, :]),
                    in0=feature_view(live["x", i][:, j, :]),
                    scalar1=live["minus_mean", i][:, j : j + 1],
                    scalar2=live["rstd", i][:, j : j + 1],
                    op0=ALU.add,
                    op1=ALU.mult,
                )
            live["normed", i] = normed

        def transpose_gain_shift(i):
            n = GROUP_TILES[i]
            normed = live["normed", i]
            h_planes = work.tile([P, CHUNKS, n * P], BF16, name="h_planes")
            for c in range(CHUNKS):
                normed_t = xt_psum.tile([P, n, P], F32, name="normed_t")
                for j in range(n):
                    nc.tensor.transpose(normed_t[:, j, :], normed[:, j, chunk_cols(c // PACK, c % PACK)], ident_f32[:])
                gain = gain_shift[:, c : c + 1]
                shift = gain_shift[:, CHUNKS + c : CHUNKS + c + 1]
                source = normed_t[:].rearrange("p j r -> p (j r)")
                if i >= GROUPS - SHARED_GROUPS and c % 2:
                    nc.vector.tensor_scalar(
                        out=h_planes[:, c, :], in0=source, scalar1=gain, scalar2=shift, op0=ALU.mult, op1=ALU.add
                    )
                else:
                    nc.scalar.activation(out=h_planes[:, c, :], in_=source, func=ACT.Identity, scale=gain, bias=shift)
            live["h_planes", i] = h_planes

        def regroup(i):
            cols = GROUP_TILES[i] * P
            vector_cols = min(cols, VECTOR_TILES * P)
            h_planes = live["h_planes", i]
            h_grouped = work.tile([P, PASSES, cols, PACK], BF16, name="h_grouped", align_bytes=64)
            for copy, g, part in (
                (nc.vector.tensor_copy, 0, slice(0, vector_cols)),
                (nc.scalar.copy, 0, slice(vector_cols, cols)),
                (nc.scalar.copy, 1, slice(0, cols)),
            ):
                if part.start < part.stop:
                    copy(
                        out=h_grouped[:, g, part, :].rearrange("p (q s) t -> p q t s", s=4),
                        in_=h_planes[:, g * PACK : (g + 1) * PACK, part].rearrange("p t (q s) -> p q t s", s=4),
                    )
            live["h_grouped", i] = h_grouped

        def quantise(i):
            cols = GROUP_TILES[i] * P
            h_codes = work.tile([P, PASSES, cols], U32, name="h_codes", align_bytes=64)
            h_scales = work.tile([P, PASSES, cols], U8, name="h_scales", align_bytes=64)
            nc.vector.quantize_mx(
                out=h_codes[:].rearrange("p g r -> p (g r)").bitcast(FP8X4),
                scales=h_scales[:].rearrange("p g r -> p (g r)"),
                in_=live["h_grouped", i][:].rearrange("p g r t -> p (g r t)"),
            )
            live["h_codes", i] = h_codes
            live["h_scales", i] = h_scales

        def project(i):
            h_codes = live["h_codes", i]
            h_scales = live["h_scales", i]
            fused = acc_psum.tile([P, GROUP_TILES[i], W], F32, name="fused")
            for j in range(GROUP_TILES[i]):
                tile_cols = slice(j * P, (j + 1) * P)
                for g in range(PASSES):
                    nc.tensor.matmul_mx(
                        out=fused[:, j, :],
                        lhsT=h_codes[:, g, tile_cols].bitcast(FP8X4),
                        lhsT_scale=h_scales[:, g, tile_cols],
                        rhs=e_codes[:, g, :].bitcast(FP8X4),
                        rhs_scale=e_scales[:, g, :],
                        start=(g == 0),
                        stop=(g == PASSES - 1),
                    )
            live["fused", i] = fused

        def finish(i):
            rows = tiles_of(i)
            nc.scalar.copy(
                out=parts[:, :, rows, :], in_=live["fused", i][:].rearrange("p j (w c) -> p w j c", w=PARTS)
            )
            for w in range(2):
                nc.sync.dma_start(out=out_rows[w][:, rows, :], in_=parts[:, w, rows, :])

        def gate(first, last):
            rows = slice(tiles_of(first).start, tiles_of(last - 1).stop)
            gelu = gate_pool.tile([P, rows.stop - rows.start, QK], F32, name="gelu")
            nc.scalar.activation(out=gelu[:], in_=parts[:, 3, rows, :], func=ACT.Gelu)
            geglu = gate_pool.tile([P, rows.stop - rows.start, QK], F32, name="geglu")
            nc.vector.tensor_tensor(out=geglu[:], in0=parts[:, 2, rows, :], in1=gelu[:], op=ALU.mult)
            nc.sync.dma_start(out=out_rows[2][:, rows, :], in_=geglu[:])

        def run(stage, i):
            if 0 <= i < GROUPS:
                stage(i)

        with tc.manual_schedule():
            for i in range(X_BUFS - 1):
                load(i)
            load_constants()
            for step in range(GROUPS + 6):
                run(load, step + X_BUFS - 1)
                run(invert, step - 1)
                run(statistics, step)
                if step == 1:
                    prepare_gain_shift()
                    sort_expand()
                run(quantise, step - 4)
                run(regroup, step - 3)
                run(normalise, step - 1)
                run(transpose_gain_shift, step - 2)
                run(deviation, step)
                if step == 2:
                    prepare_expand()
                run(project, step - 5)
                run(finish, step - 6)
                if step == GROUPS + 3:
                    gate(0, EARLY_GATES // 2)
                    gate(EARLY_GATES // 2, EARLY_GATES)
            gate(EARLY_GATES, GROUPS)
